import numpy as np
import ml_dtypes


def mxq(x, axis, fmt="e4m3"):
    dtype, down = {"e4m3": (ml_dtypes.float8_e4m3fn, 7), "e5m2": (ml_dtypes.float8_e5m2, 14)}[fmt]
    v = np.moveaxis(np.asarray(x, np.float32).astype(ml_dtypes.bfloat16).astype(np.float64), axis, -1)
    blocks = v.reshape(v.shape[:-1] + (-1, 32))
    amax = np.abs(blocks).max(-1, keepdims=True)
    byte = np.maximum(np.where(amax > 0, np.frexp(amax)[1] - 1 + 127, 0) - down, 1)
    scale = np.exp2(byte - 127.0)
    codes = (blocks / scale).astype(np.float32).astype(dtype).astype(np.float64)
    return np.moveaxis((codes * scale).reshape(v.shape), -1, axis)


WIDE = False


def mx_kscale(k):
    if not WIDE:
        return np.ones(k)
    levels = np.array([10, -10, 5, -5, 0])
    a = np.random.permutation(np.resize(levels, k // 512 * 4)).reshape(k // 512, 4)
    idx = np.arange(k)
    return np.exp2(a[idx // 512, idx % 128 // 32])


BF16 = ml_dtypes.bfloat16


def bf(x):
    return np.asarray(x, np.float32).astype(BF16)


def f64(x):
    return np.asarray(x).astype(np.float64)


E2M1 = np.array([0.0, 0.5, 1.0, 1.5, 2.0, 3.0, 4.0, 6.0, -0.0, -0.5, -1.0, -1.5, -2.0, -3.0, -4.0, -6.0])


def pack_weight(w, fmt):
    k, n = w.shape
    w = f64(bf(w)).reshape(k // 32, 32, n)
    amax = np.abs(w).max(1)
    if fmt == "e4m3":
        byte = np.frexp(amax)[1] - 1 + 127 - 7
    else:
        mant, ex = np.frexp(amax / 6.0)
        byte = np.where(mant > 0.5, ex, ex - 1) + 127
    byte = np.clip(np.where(amax > 0, byte, 1), 1, 254)
    scaled = (w * np.exp2(127.0 - byte)[:, None, :]).reshape(k, n).astype(np.float32)
    by_word = np.ascontiguousarray(scaled.reshape(k // 512, 128, 4, n).transpose(0, 1, 3, 2))
    if fmt == "e4m3":
        words = by_word.astype(ml_dtypes.float8_e4m3fn).view(np.uint8)
    else:
        c = by_word.astype(ml_dtypes.float4_e2m1fn).view(np.uint8) & 0xF
        words = c[..., 0::2] | (c[..., 1::2] << 4)
    return np.ascontiguousarray(words), np.ascontiguousarray(byte.astype(np.uint8).reshape(k // 512, 16, n))


def unpack_weight(words, scales, fmt):
    g, p, n, _ = words.shape
    if fmt == "e4m3":
        vals = np.ascontiguousarray(words).view(ml_dtypes.float8_e4m3fn).astype(np.float64)
    else:
        nib = np.empty((g, p, n, 4), np.uint8)
        nib[..., 0::2] = words & 0xF
        nib[..., 1::2] = words >> 4
        vals = E2M1[nib]
    vals = vals * np.repeat(np.exp2(scales.astype(np.float64) - 127.0), 8, axis=1)[..., None]
    return vals.transpose(0, 1, 3, 2).reshape(g * 512, n)


B, I, H = 4096, 1024, 256
G = 3
QH = H % 2 ** 9 == 0


def sigmoid(v):
    return 1.0 / (1.0 + np.exp(-v))


def setup_inputs():
    s = mx_kscale(I)
    x = bf(np.random.standard_normal((B, I)) * s)
    hid = bf(np.random.standard_normal((B, H)))
    wx = np.random.standard_normal((G, I, H)) * 0.6 / np.sqrt(I) / s[None, :, None]
    wx_words, wx_scales = pack_weight(wx.reshape(-1, H), "e4m3")
    wh = bf(np.random.standard_normal((3, H, H)) * 0.6 / np.sqrt(H))
    bx = bf(np.random.standard_normal((3, H)) * 0.3)
    bh = bf(np.random.standard_normal((3, H)) * 0.3)
    return {"x": x,
            "hid": hid,
            "wx_words": wx_words,
            "wx_scales": wx_scales,
            "wh": wh,
            "bx": bx,
            "bh": bh}


def reference(x, hid, wx_words, wx_scales, wh, bx, bh):
    x, hid, wh, bx, bh = f64(x), f64(hid), f64(wh), f64(bx), f64(bh)
    px = mxq(x, 1, "e4m3") @ unpack_weight(wx_words, wx_scales, "e4m3").reshape(G, I, H)
    if QH:
        ph = mxq(hid, 1, "e4m3") @ mxq(wh, 1, "e4m3")
    else:
        ph = hid @ wh
    gx = px.transpose(1, 0, 2) + bx[None]
    gh = ph.transpose(1, 0, 2) + bh[None]
    r = sigmoid(gx[:, 0] + gh[:, 0])
    z = sigmoid(gx[:, 1] + gh[:, 1])
    n = np.tanh(gx[:, 2] + r * gh[:, 2])
    next_hid = (1.0 - z) * n + z * hid
    return next_hid

@@ -1,0 +1,264 @@
+from contextlib import ExitStack
+
+import concourse.mybir as mybir
+from concourse.masks import make_identity
+
+F32 = mybir.dt.float32
+BF16 = mybir.dt.bfloat16
+I32 = mybir.dt.int32
+U32 = mybir.dt.uint32
+U8 = mybir.dt.uint8
+FP8X4 = mybir.dt.float8_e4m3fn_x4
+ACT = mybir.ActivationFunctionType
+ALU = mybir.AluOpType
+
+P = 128
+PACK = 4
+K_PASS = P * PACK
+
+BATCH, N_IN, N_HID = 4096, 1024, 256
+GATE_R, GATE_Z, GATE_N = 0, 1, 2
+GATES = 3
+X_PASSES = N_IN // K_PASS
+HALVES = N_HID // P
+CHUNK = 512
+TILES = CHUNK // P
+N_CHUNKS = BATCH // CHUNK
+PAIRS = TILES // 2
+BLEND_LAG = 2
+
+FLOPS = 2 * BATCH * (N_IN + N_HID) * GATES * N_HID
+
+
+def tile_grucellv2_t_e_kernel(tc, x, hid, wx_words, wx_scales, wh, bx, bh, out):
+    nc = tc.nc
+    x_chunks = x.rearrange("(c p s) k -> c p s k", p=P, s=TILES)
+    hid_chunks = hid.rearrange("(c p s) h -> c p s h", p=P, s=TILES)
+    out_chunks = out.rearrange("(c p s) h -> c p s h", p=P, s=TILES)
+
+    with ExitStack() as ctx:
+        consts = ctx.enter_context(tc.tile_pool(name="consts", bufs=1))
+        inputs = ctx.enter_context(tc.tile_pool(name="inputs", bufs=N_CHUNKS))
+        work = ctx.enter_context(tc.tile_pool(name="work", bufs=3))
+        psum_mm = ctx.enter_context(tc.psum_pool(name="psum_mm", bufs=2))
+        psum_tr = ctx.enter_context(tc.psum_pool(name="psum_tr", bufs=3))
+        psum_hid = ctx.enter_context(tc.psum_pool(name="psum_hid", bufs=1))
+        ctx.enter_context(tc.manual_schedule())
+
+        x_rows, hid_rows = {}, {}
+        x_grouped, x_codes, x_scales = {}, {}, {}
+        hid_bank, hid_t = {}, {}
+        gate_t = {}
+        out_t, out_rows = {}, {}
+
+        def load_chunk(c):
+            hid_rows[c] = inputs.tile([P, TILES, N_HID], BF16, name="hid_rows%d" % c, tag="hid_rows")
+            nc.sync.dma_start(out=hid_rows[c][:], in_=hid_chunks[c])
+            x_rows[c] = inputs.tile([P, TILES, N_IN], BF16, name="x_rows%d" % c, tag="x_rows")
+            for g in range(X_PASSES):
+                columns = slice(K_PASS * g, K_PASS * (g + 1))
+                nc.sync.dma_start(out=x_rows[c][:, :, columns], in_=x_chunks[c][:, :, columns])
+
+        load_chunk(0)
+
+        wh_sb = consts.tile([P, GATES * HALVES, N_HID], BF16)
+        nc.sync.dma_start(out=wh_sb[:], in_=wh.rearrange("g (k p) n -> p (g k) n", p=P))
+
+        w_scales = consts.tile([P, GATES * X_PASSES, N_HID], U8, align_bytes=64)
+        nc.vector.memset(w_scales[:].rearrange("p g n -> p (g n)").bitcast(I32), 0)
+        for quadrant in range(4):
+            nc.sync.dma_start(
+                out=w_scales[32 * quadrant : 32 * quadrant + 4, :, :].bitcast(I32),
+                in_=wx_scales[:, 4 * quadrant : 4 * quadrant + 4, :].rearrange("g r n -> r g n").bitcast(I32),
+            )
+        w_codes = consts.tile([P, GATES * X_PASSES, N_HID], U32, align_bytes=64)
+        nc.sync.dma_start(
+            out=w_codes[:].bitcast(I32),
+            in_=wx_words.rearrange("g p n t -> p g (n t)").bitcast(I32),
+        )
+
+        bias_rows = consts.tile([P, P], BF16)
+        nc.vector.memset(bias_rows[:], 0.0)
+        nc.sync.dma_start(out=bias_rows[0:6, :], in_=bx.rearrange("g (j p) -> (g j) p", p=P))
+        nc.sync.dma_start(out=bias_rows[6:12, :], in_=bh.rearrange("g (j p) -> (g j) p", p=P))
+
+        for c in range(1, N_CHUNKS):
+            load_chunk(c)
+
+        ident_bf16 = consts.tile([P, P], BF16)
+        make_identity(nc, ident_bf16[:])
+        ident_f32 = consts.tile([P, P], F32)
+        make_identity(nc, ident_f32[:])
+
+        def begin_transposing(c):
+            x_codes[c] = work.tile([P, X_PASSES, CHUNK], U32, name="x_codes%d" % c, tag="x_codes", align_bytes=64)
+            x_scales[c] = work.tile([P, X_PASSES, CHUNK], U8, name="x_scales%d" % c, tag="x_scales", align_bytes=64)
+            hid_bank[c] = psum_hid.tile([P, HALVES, CHUNK], BF16, name="hid_bank%d" % c, tag="hid_bank")
+
+        def transpose_x_tile(c, g, s, bank):
+            words = x_rows[c][:].bitcast(F32)
+            for u in range(2):
+                nc.tensor.transpose(
+                    out=bank[:, s % 2, u, :],
+                    in_=words[:, s, 256 * g + u : 256 * (g + 1) : 2],
+                    identity=ident_f32[:],
+                )
+
+        def regroup_x_pair(c, g, pair, bank):
+            if pair == 0:
+                x_grouped[(c, g)] = work.tile(
+                    [P, CHUNK * PACK], BF16, name="x_grouped%d_%d" % (c, g), tag="x_grouped", bufs=4, align_bytes=64
+                )
+            words = x_grouped[(c, g)][:].bitcast(F32)[:, 512 * pair : 512 * (pair + 1)]
+            nc.vector.tensor_copy(
+                out=words.rearrange("p (k b u) -> p k b u", k=2, u=2),
+                in_=bank[:].rearrange("p k u b -> p k b u"),
+            )
+
+        def quantise_x(c, g):
+            nc.vector.quantize_mx(
+                out=x_codes[c][:, g, :].bitcast(FP8X4),
+                scales=x_scales[c][:, g, :],
+                in_=x_grouped[(c, g)][:],
+            )
+
+        def transpose_hid_tile(c, s, half):
+            nc.tensor.transpose(
+                out=hid_bank[c][:, half, P * s : P * (s + 1)],
+                in_=hid_rows[c][:, s, P * half : P * (half + 1)],
+                identity=ident_bf16[:],
+            )
+
+        def keep_hid_t(c):
+            hid_t[c] = work.tile([P, HALVES, CHUNK], BF16, name="hid_t%d" % c, tag="hid_t", bufs=4)
+            nc.scalar.copy(out=hid_t[c][:], in_=hid_bank[c][:])
+
+        def transpose_out_tile(c, s, bank):
+            for half in range(HALVES):
+                nc.tensor.transpose(
+                    out=bank[:, s % 2, P * half : P * (half + 1)],
+                    in_=out_t[c][:, half, P * s : P * (s + 1)],
+                    identity=ident_f32[:],
+                )
+
+        def keep_out_pair(c, pair, bank):
+            if pair == 0:
+                out_rows[c] = work.tile([P, TILES, N_HID], F32, name="out_rows%d" % c, tag="out_rows")
+            rows = slice(2 * pair, 2 * pair + 2)
+            nc.scalar.copy(out=out_rows[c][:, rows, :], in_=bank[:])
+            nc.sync.dma_start(out=out_chunks[c][:, rows, :], in_=out_rows[c][:, rows, :])
+
+        begin_transposing(0)
+        for s in range(TILES):
+            for half in range(HALVES):
+                transpose_hid_tile(0, s, half)
+        keep_hid_t(0)
+        for g in range(X_PASSES):
+            for pair in range(PAIRS):
+                x_bank = psum_tr.tile([P, 2, 2, P], F32, name="x_bank", tag="bank")
+                for k in range(2):
+                    transpose_x_tile(0, g, 2 * pair + k, x_bank)
+                regroup_x_pair(0, g, pair, x_bank)
+        for g in range(X_PASSES):
+            quantise_x(0, g)
+
+        bias_bank = psum_tr.tile([P, P], BF16, name="bias_bank", tag="bank")
+        nc.tensor.transpose(out=bias_bank[:], in_=bias_rows[:], identity=ident_bf16[:])
+        bias = consts.tile([P, 2 * GATES * HALVES], F32)
+        nc.vector.tensor_copy(out=bias[:], in_=bias_bank[:, 0 : 2 * GATES * HALVES])
+        bias_x = bias[:, 0 : GATES * HALVES]
+        bias_h = bias[:, GATES * HALVES : 2 * GATES * HALVES]
+        bias_sum = consts.tile([P, GATES * HALVES], F32)
+        nc.vector.tensor_add(out=bias_sum[:], in0=bias_x, in1=bias_h)
+
+        for c in range(N_CHUNKS):
+            ahead = c + 1
+            behind = c - BLEND_LAG
+            if ahead < N_CHUNKS:
+                begin_transposing(ahead)
+            for gate in range(GATES):
+                gate_t[(c, gate)] = work.tile([P, HALVES, CHUNK], F32, name="gate%d_%d" % (gate, c), tag="gate%d" % gate)
+                h_sum, x_sum, h_part = [], [], []
+
+                for j in range(HALVES):
+                    h_sum.append(psum_mm.tile([P, CHUNK], F32, name="h_sum", tag="h_sum"))
+                    weave_x = gate != GATE_N and ahead < N_CHUNKS
+                    weave_out = gate == GATE_N and behind >= 0
+                    if weave_x:
+                        bank = psum_tr.tile([P, 2, 2, P], F32, name="x_bank", tag="bank")
+                    if weave_out:
+                        bank = psum_tr.tile([P, 2, N_HID], F32, name="out_bank", tag="bank")
+                    for k in range(HALVES):
+                        nc.tensor.matmul(
+                            out=h_sum[j][:],
+                            lhsT=wh_sb[:, HALVES * gate + k, P * j : P * (j + 1)],
+                            rhs=hid_t[c][:, k, :],
+                            start=(k == 0),
+                            stop=(k == HALVES - 1),
+                        )
+                        if weave_x:
+                            transpose_x_tile(ahead, gate, 2 * j + k, bank)
+                            transpose_hid_tile(ahead, 2 * gate + j, k)
+                        if weave_out:
+                            transpose_out_tile(behind, 2 * j + k, bank)
+                    if weave_x:
+                        regroup_x_pair(ahead, gate, j, bank)
+                    if weave_out:
+                        keep_out_pair(behind, j, bank)
+
+                for j in range(HALVES):
+                    h_part.append(work.tile([P, CHUNK], F32, name="h_part", tag="h_part", bufs=4))
+                    if gate == GATE_N:
+                        nc.vector.scalar_tensor_tensor(
+                            out=h_part[j][:],
+                            in0=h_sum[j][:],
+                            scalar=bias_h[:, HALVES * GATE_N + j : HALVES * GATE_N + j + 1],
+                            in1=gate_t[(c, GATE_R)][:, j, :],
+                            op0=ALU.add,
+                            op1=ALU.mult,
+                        )
+                    else:
+                        nc.scalar.copy(out=h_part[j][:], in_=h_sum[j][:])
+                if gate == GATE_Z and ahead < N_CHUNKS:
+                    keep_hid_t(ahead)
+
+                for j in range(HALVES):
+                    x_sum.append(psum_mm.tile([P, CHUNK], F32, name="x_sum", tag="x_sum"))
+                    for g in range(X_PASSES):
+                        nc.tensor.matmul_mx(
+                            out=x_sum[j][:],
+                            lhsT=w_codes[:, X_PASSES * gate + g, P * j : P * (j + 1)].bitcast(FP8X4),
+                            lhsT_scale=w_scales[:, X_PASSES * gate + g, P * j : P * (j + 1)],
+                            rhs=x_codes[c][:, g, :].bitcast(FP8X4),
+                            rhs_scale=x_scales[c][:, g, :],
+                            start=(g == 0),
+                            stop=(g == X_PASSES - 1),
+                        )
+
+                for j in range(HALVES):
+                    nc.vector.tensor_tensor(
+                        out=gate_t[(c, gate)][:, j, :], in0=x_sum[j][:], in1=h_part[j][:], op=ALU.add
+                    )
+                for j in range(HALVES):
+                    column = HALVES * gate + j
+                    nc.scalar.activation(
+                        out=gate_t[(c, gate)][:, j, :],
+                        in_=gate_t[(c, gate)][:, j, :],
+                        func=ACT.Tanh if gate == GATE_N else ACT.Sigmoid,
+                        bias=bias_x[:, column : column + 1] if gate == GATE_N else bias_sum[:, column : column + 1],
+                    )
+                if gate != GATE_N and ahead < N_CHUNKS:
+                    quantise_x(ahead, gate)
+
+            blender = nc.vector if c == N_CHUNKS - 1 else nc.gpsimd
+            out_t[c] = work.tile([P, HALVES, CHUNK], F32, name="out_t%d" % c, tag="out_t")
+            blender.tensor_tensor(out=out_t[c][:], in0=hid_t[c][:], in1=gate_t[(c, GATE_N)][:], op=ALU.subtract)
+            blender.tensor_tensor(out=out_t[c][:], in0=gate_t[(c, GATE_Z)][:], in1=out_t[c][:], op=ALU.mult)
+            blender.tensor_tensor(out=out_t[c][:], in0=gate_t[(c, GATE_N)][:], in1=out_t[c][:], op=ALU.add)
+
+        for c in range(N_CHUNKS - BLEND_LAG, N_CHUNKS):
+            for pair in range(PAIRS):
+                out_bank = psum_tr.tile([P, 2, N_HID], F32, name="out_bank", tag="bank")
+                for k in range(2):
+                    transpose_out_tile(c, 2 * pair + k, out_bank)
+                keep_out_pair(c, pair, out_bank)

@@ -110,7 +110,7 @@ def tile_grucellv2_t_e_kernel(tc, x, hid, wx_words, wx_scales, wh, bx, bh, out):
                     [P, CHUNK * PACK], BF16, name="x_grouped%d_%d" % (c, g), tag="x_grouped", bufs=4, align_bytes=64
                 )
             words = x_grouped[(c, g)][:].bitcast(F32)[:, 512 * pair : 512 * (pair + 1)]
-            nc.vector.tensor_copy(
+            nc.scalar.copy(
                 out=words.rearrange("p (k b u) -> p k b u", k=2, u=2),
                 in_=bank[:].rearrange("p k u b -> p k b u"),
             )
@@ -218,7 +218,7 @@ def tile_grucellv2_t_e_kernel(tc, x, hid, wx_words, wx_scales, wh, bx, bh, out):
                             op1=ALU.mult,
                         )
                     else:
-                        nc.scalar.copy(out=h_part[j][:], in_=h_sum[j][:])
+                        nc.vector.tensor_copy(out=h_part[j][:], in_=h_sum[j][:])
                 if gate == GATE_Z and ahead < N_CHUNKS:
                     keep_hid_t(ahead)
 

@@ -51,39 +51,63 @@ def tile_grucellv2_t_e_kernel(tc, x, hid, wx_words, wx_scales, wh, bx, bh, out):
         gate_t = {}
         out_t, out_rows = {}, {}
 
-        def load_chunk(c):
+        def load_hid(c):
             hid_rows[c] = inputs.tile([P, TILES, N_HID], BF16, name="hid_rows%d" % c, tag="hid_rows")
             nc.sync.dma_start(out=hid_rows[c][:], in_=hid_chunks[c])
+
+        def load_x(c):
             x_rows[c] = inputs.tile([P, TILES, N_IN], BF16, name="x_rows%d" % c, tag="x_rows")
             for g in range(X_PASSES):
                 columns = slice(K_PASS * g, K_PASS * (g + 1))
                 nc.sync.dma_start(out=x_rows[c][:, :, columns], in_=x_chunks[c][:, :, columns])
 
-        load_chunk(0)
+        def load_x_part(c, g, pair):
+            rows, columns = slice(2 * pair, 2 * pair + 2), slice(K_PASS * g, K_PASS * (g + 1))
+            nc.sync.dma_start(out=x_rows[c][:, rows, columns], in_=x_chunks[c][:, rows, columns])
 
-        wh_sb = consts.tile([P, GATES * HALVES, N_HID], BF16)
-        nc.sync.dma_start(out=wh_sb[:], in_=wh.rearrange("g (k p) n -> p (g k) n", p=P))
-
-        w_scales = consts.tile([P, GATES * X_PASSES, N_HID], U8, align_bytes=64)
-        nc.vector.memset(w_scales[:].rearrange("p g n -> p (g n)").bitcast(I32), 0)
-        for quadrant in range(4):
+        def load_codes(gate):
+            groups = slice(X_PASSES * gate, X_PASSES * (gate + 1))
             nc.sync.dma_start(
-                out=w_scales[32 * quadrant : 32 * quadrant + 4, :, :].bitcast(I32),
-                in_=wx_scales[:, 4 * quadrant : 4 * quadrant + 4, :].rearrange("g r n -> r g n").bitcast(I32),
+                out=w_codes[:, groups, :].bitcast(I32),
+                in_=wx_words[groups].rearrange("g p n t -> p g (n t)").bitcast(I32),
             )
-        w_codes = consts.tile([P, GATES * X_PASSES, N_HID], U32, align_bytes=64)
-        nc.sync.dma_start(
-            out=w_codes[:].bitcast(I32),
-            in_=wx_words.rearrange("g p n t -> p g (n t)").bitcast(I32),
-        )
 
         bias_rows = consts.tile([P, P], BF16)
         nc.vector.memset(bias_rows[:], 0.0)
-        nc.sync.dma_start(out=bias_rows[0:6, :], in_=bx.rearrange("g (j p) -> (g j) p", p=P))
-        nc.sync.dma_start(out=bias_rows[6:12, :], in_=bh.rearrange("g (j p) -> (g j) p", p=P))
 
-        for c in range(1, N_CHUNKS):
-            load_chunk(c)
+        def load_biases():
+            nc.sync.dma_start(out=bias_rows[0:6, :], in_=bx.rearrange("g (j p) -> (g j) p", p=P))
+            nc.sync.dma_start(out=bias_rows[6:12, :], in_=bh.rearrange("g (j p) -> (g j) p", p=P))
+
+        w_scales = consts.tile([P, GATES * X_PASSES, N_HID], U8, align_bytes=64)
+        nc.vector.memset(w_scales[:].rearrange("p g n -> p (g n)").bitcast(I32), 0)
+        w_codes = consts.tile([P, GATES * X_PASSES, N_HID], U32, align_bytes=64)
+        wh_sb = consts.tile([P, GATES * HALVES, N_HID], BF16)
+
+        def load_scales():
+            for quadrant in range(4):
+                nc.sync.dma_start(
+                    out=w_scales[32 * quadrant : 32 * quadrant + 4, :, :].bitcast(I32),
+                    in_=wx_scales[:, 4 * quadrant : 4 * quadrant + 4, :].rearrange("g r n -> r g n").bitcast(I32),
+                )
+
+        load_hid(0)
+        x_rows[0] = inputs.tile([P, TILES, N_IN], BF16, name="x_rows0", tag="x_rows")
+        for g in range(X_PASSES):
+            for pair in range(PAIRS):
+                load_x_part(0, g, pair)
+        nc.sync.dma_start(out=wh_sb[:], in_=wh.rearrange("g (k p) n -> p (g k) n", p=P))
+        load_codes(GATE_R)
+        load_scales()
+        load_biases()
+        load_codes(GATE_Z)
+        load_hid(1)
+        load_x(1)
+        load_codes(GATE_N)
+
+        for c in range(2, N_CHUNKS):
+            load_hid(c)
+            load_x(c)
 
         ident_bf16 = consts.tile([P, P], BF16)
         make_identity(nc, ident_bf16[:])
@@ -104,13 +128,13 @@ def tile_grucellv2_t_e_kernel(tc, x, hid, wx_words, wx_scales, wh, bx, bh, out):
                     identity=ident_f32[:],
                 )
 
-        def regroup_x_pair(c, g, pair, bank):
+        def regroup_x_pair(c, g, pair, bank, copy=nc.scalar.copy):
             if pair == 0:
                 x_grouped[(c, g)] = work.tile(
                     [P, CHUNK * PACK], BF16, name="x_grouped%d_%d" % (c, g), tag="x_grouped", bufs=4, align_bytes=64
                 )
             words = x_grouped[(c, g)][:].bitcast(F32)[:, 512 * pair : 512 * (pair + 1)]
-            nc.scalar.copy(
+            copy(
                 out=words.rearrange("p (k b u) -> p k b u", k=2, u=2),
                 in_=bank[:].rearrange("p k u b -> p k b u"),
             )
@@ -129,9 +153,9 @@ def tile_grucellv2_t_e_kernel(tc, x, hid, wx_words, wx_scales, wh, bx, bh, out):
                 identity=ident_bf16[:],
             )
 
-        def keep_hid_t(c):
+        def keep_hid_t(c, copy=nc.scalar.copy):
             hid_t[c] = work.tile([P, HALVES, CHUNK], BF16, name="hid_t%d" % c, tag="hid_t", bufs=4)
-            nc.scalar.copy(out=hid_t[c][:], in_=hid_bank[c][:])
+            copy(out=hid_t[c][:], in_=hid_bank[c][:])
 
         def transpose_out_tile(c, s, bank):
             for half in range(HALVES):
@@ -141,6 +165,68 @@ def tile_grucellv2_t_e_kernel(tc, x, hid, wx_words, wx_scales, wh, bx, bh, out):
                     identity=ident_f32[:],
                 )
 
+        def bias_column(gate, j):
+            column = HALVES * gate + j
+            return (bias_x if gate == GATE_N else bias_sum)[:, column : column + 1]
+
+        def plain_half(c, gate, j, behind_matmul):
+            bank = psum_mm.tile([P, CHUNK], F32, name="h_sum", tag="h_sum")
+            for k in range(HALVES):
+                nc.tensor.matmul(
+                    out=bank[:],
+                    lhsT=wh_sb[:, HALVES * gate + k, P * j : P * (j + 1)],
+                    rhs=hid_t[c][:, k, :],
+                    start=(k == 0),
+                    stop=(k == HALVES - 1),
+                )
+                behind_matmul(k)
+            return bank
+
+        def plain_part(c, gate, j, bank, copy=nc.vector.tensor_copy):
+            part = work.tile([P, CHUNK], F32, name="h_part", tag="h_part", bufs=4)
+            if gate == GATE_N:
+                nc.vector.scalar_tensor_tensor(
+                    out=part[:],
+                    in0=bank[:],
+                    scalar=bias_h[:, HALVES * GATE_N + j : HALVES * GATE_N + j + 1],
+                    in1=gate_t[(c, GATE_R)][:, j, :],
+                    op0=ALU.add,
+                    op1=ALU.mult,
+                )
+            else:
+                copy(out=part[:], in_=bank[:])
+            return part
+
+        def mx_half(c, gate, j):
+            bank = psum_mm.tile([P, CHUNK], F32, name="x_sum", tag="x_sum")
+            for g in range(X_PASSES):
+                nc.tensor.matmul_mx(
+                    out=bank[:],
+                    lhsT=w_codes[:, X_PASSES * gate + g, P * j : P * (j + 1)].bitcast(FP8X4),
+                    lhsT_scale=w_scales[:, X_PASSES * gate + g, P * j : P * (j + 1)],
+                    rhs=x_codes[c][:, g, :].bitcast(FP8X4),
+                    rhs_scale=x_scales[c][:, g, :],
+                    start=(g == 0),
+                    stop=(g == X_PASSES - 1),
+                )
+            return bank
+
+        def add_half(c, gate, j, bank, part):
+            nc.vector.tensor_tensor(out=gate_t[(c, gate)][:, j, :], in0=bank[:], in1=part[:], op=ALU.add)
+
+        def activate_half(c, gate, j):
+            nc.scalar.activation(
+                out=gate_t[(c, gate)][:, j, :],
+                in_=gate_t[(c, gate)][:, j, :],
+                func=ACT.Tanh if gate == GATE_N else ACT.Sigmoid,
+                bias=bias_column(gate, j),
+            )
+
+        def blend(c, engine, part):
+            engine.tensor_tensor(out=out_t[c][:, part, :], in0=hid_t[c][:, part, :], in1=gate_t[(c, GATE_N)][:, part, :], op=ALU.subtract)
+            engine.tensor_tensor(out=out_t[c][:, part, :], in0=gate_t[(c, GATE_Z)][:, part, :], in1=out_t[c][:, part, :], op=ALU.mult)
+            engine.tensor_tensor(out=out_t[c][:, part, :], in0=gate_t[(c, GATE_N)][:, part, :], in1=out_t[c][:, part, :], op=ALU.add)
+
         def keep_out_pair(c, pair, bank):
             if pair == 0:
                 out_rows[c] = work.tile([P, TILES, N_HID], F32, name="out_rows%d" % c, tag="out_rows")
@@ -148,20 +234,20 @@ def tile_grucellv2_t_e_kernel(tc, x, hid, wx_words, wx_scales, wh, bx, bh, out):
             nc.scalar.copy(out=out_rows[c][:, rows, :], in_=bank[:])
             nc.sync.dma_start(out=out_chunks[c][:, rows, :], in_=out_rows[c][:, rows, :])
 
+        V, S = nc.vector.tensor_copy, nc.scalar.copy
         begin_transposing(0)
         for s in range(TILES):
             for half in range(HALVES):
                 transpose_hid_tile(0, s, half)
-        keep_hid_t(0)
+        keep_hid_t(0, S)
+        engines0 = (S, V, S, V)
         for g in range(X_PASSES):
             for pair in range(PAIRS):
                 x_bank = psum_tr.tile([P, 2, 2, P], F32, name="x_bank", tag="bank")
                 for k in range(2):
                     transpose_x_tile(0, g, 2 * pair + k, x_bank)
-                regroup_x_pair(0, g, pair, x_bank)
-        for g in range(X_PASSES):
+                regroup_x_pair(0, g, pair, x_bank, engines0[2 * g + pair])
             quantise_x(0, g)
-
         bias_bank = psum_tr.tile([P, P], BF16, name="bias_bank", tag="bank")
         nc.tensor.transpose(out=bias_bank[:], in_=bias_rows[:], identity=ident_bf16[:])
         bias = consts.tile([P, 2 * GATES * HALVES], F32)
@@ -171,94 +257,91 @@ def tile_grucellv2_t_e_kernel(tc, x, hid, wx_words, wx_scales, wh, bx, bh, out):
         bias_sum = consts.tile([P, GATES * HALVES], F32)
         nc.vector.tensor_add(out=bias_sum[:], in0=bias_x, in1=bias_h)
 
+        LAST = N_CHUNKS - 1
         for c in range(N_CHUNKS):
             ahead = c + 1
-            behind = c - BLEND_LAG
             if ahead < N_CHUNKS:
                 begin_transposing(ahead)
+            weave_x = {GATE_N: 0} if c == 0 else {GATE_R: 0, GATE_Z: 1}
+            weave_hid = {GATE_Z: (0, 1)} if c == 0 else {GATE_R: (0,), GATE_Z: (1,)}
+            if ahead >= N_CHUNKS:
+                weave_x, weave_hid = {}, {}
+            weave_out = {GATE_N: c - BLEND_LAG}
+            if c == LAST:
+                weave_out = {GATE_Z: c - 2}
             for gate in range(GATES):
                 gate_t[(c, gate)] = work.tile([P, HALVES, CHUNK], F32, name="gate%d_%d" % (gate, c), tag="gate%d" % gate)
                 h_sum, x_sum, h_part = [], [], []
-
+                back = weave_out.get(gate, -1)
+                mx_first = False
+                if mx_first:
+                    for j in range(HALVES):
+                        x_sum.append(mx_half(c, gate, j))
                 for j in range(HALVES):
-                    h_sum.append(psum_mm.tile([P, CHUNK], F32, name="h_sum", tag="h_sum"))
-                    weave_x = gate != GATE_N and ahead < N_CHUNKS
-                    weave_out = gate == GATE_N and behind >= 0
-                    if weave_x:
-                        bank = psum_tr.tile([P, 2, 2, P], F32, name="x_bank", tag="bank")
-                    if weave_out:
-                        bank = psum_tr.tile([P, 2, N_HID], F32, name="out_bank", tag="bank")
-                    for k in range(HALVES):
-                        nc.tensor.matmul(
-                            out=h_sum[j][:],
-                            lhsT=wh_sb[:, HALVES * gate + k, P * j : P * (j + 1)],
-                            rhs=hid_t[c][:, k, :],
-                            start=(k == 0),
-                            stop=(k == HALVES - 1),
-                        )
-                        if weave_x:
-                            transpose_x_tile(ahead, gate, 2 * j + k, bank)
-                            transpose_hid_tile(ahead, 2 * gate + j, k)
-                        if weave_out:
-                            transpose_out_tile(behind, 2 * j + k, bank)
-                    if weave_x:
-                        regroup_x_pair(ahead, gate, j, bank)
-                    if weave_out:
-                        keep_out_pair(behind, j, bank)
+                    x_bank = out_bank = None
+                    if gate in weave_x:
+                        x_bank = psum_tr.tile([P, 2, 2, P], F32, name="x_bank", tag="bank")
+                    if back >= 0:
+                        out_bank = psum_tr.tile([P, 2, N_HID], F32, name="out_bank", tag="bank")
 
+                    def behind_matmul(k):
+                        if gate in weave_x:
+                            transpose_x_tile(ahead, weave_x[gate], 2 * j + k, x_bank)
+                        for i in weave_hid.get(gate, ()):
+                            transpose_hid_tile(ahead, 2 * i + j, k)
+                        if back >= 0:
+                            transpose_out_tile(back, 2 * j + k, out_bank)
+
+                    h_sum.append(plain_half(c, gate, j, behind_matmul))
+                    if gate in weave_x:
+                        regroup_x_pair(ahead, weave_x[gate], j, x_bank)
+                    if back >= 0:
+                        keep_out_pair(back, j, out_bank)
                 for j in range(HALVES):
-                    h_part.append(work.tile([P, CHUNK], F32, name="h_part", tag="h_part", bufs=4))
-                    if gate == GATE_N:
-                        nc.vector.scalar_tensor_tensor(
-                            out=h_part[j][:],
-                            in0=h_sum[j][:],
-                            scalar=bias_h[:, HALVES * GATE_N + j : HALVES * GATE_N + j + 1],
-                            in1=gate_t[(c, GATE_R)][:, j, :],
-                            op0=ALU.add,
-                            op1=ALU.mult,
-                        )
-                    else:
-                        nc.vector.tensor_copy(out=h_part[j][:], in_=h_sum[j][:])
+                    h_part.append(plain_part(c, gate, j, h_sum[j], S if c == 0 and gate in (GATE_R,) else V))
                 if gate == GATE_Z and ahead < N_CHUNKS:
                     keep_hid_t(ahead)
+                if not mx_first:
+                    for j in range(HALVES):
+                        x_sum.append(mx_half(c, gate, j))
+                if c == 0 and gate == GATE_N:
+                    for pair in range(PAIRS):
+                        x_bank = psum_tr.tile([P, 2, 2, P], F32, name="x_bank", tag="bank")
+                        for k in range(2):
+                            transpose_x_tile(1, 1, 2 * pair + k, x_bank)
+                        regroup_x_pair(1, 1, pair, x_bank, S)
+                for j in range(HALVES):
+                    add_half(c, gate, j, x_sum[j], h_part[j])
 
                 for j in range(HALVES):
-                    x_sum.append(psum_mm.tile([P, CHUNK], F32, name="x_sum", tag="x_sum"))
-                    for g in range(X_PASSES):
-                        nc.tensor.matmul_mx(
-                            out=x_sum[j][:],
-                            lhsT=w_codes[:, X_PASSES * gate + g, P * j : P * (j + 1)].bitcast(FP8X4),
-                            lhsT_scale=w_scales[:, X_PASSES * gate + g, P * j : P * (j + 1)],
-                            rhs=x_codes[c][:, g, :].bitcast(FP8X4),
-                            rhs_scale=x_scales[c][:, g, :],
-                            start=(g == 0),
-                            stop=(g == X_PASSES - 1),
-                        )
+                    activate_half(c, gate, j)
+                if gate in weave_x:
+                    quantise_x(ahead, weave_x[gate])
+                if c == 0 and gate == GATE_N:
+                    quantise_x(1, 1)
 
-                for j in range(HALVES):
-                    nc.vector.tensor_tensor(
-                        out=gate_t[(c, gate)][:, j, :], in0=x_sum[j][:], in1=h_part[j][:], op=ALU.add
-                    )
-                for j in range(HALVES):
-                    column = HALVES * gate + j
-                    nc.scalar.activation(
-                        out=gate_t[(c, gate)][:, j, :],
-                        in_=gate_t[(c, gate)][:, j, :],
-                        func=ACT.Tanh if gate == GATE_N else ACT.Sigmoid,
-                        bias=bias_x[:, column : column + 1] if gate == GATE_N else bias_sum[:, column : column + 1],
-                    )
-                if gate != GATE_N and ahead < N_CHUNKS:
-                    quantise_x(ahead, gate)
-
-            blender = nc.vector if c == N_CHUNKS - 1 else nc.gpsimd
             out_t[c] = work.tile([P, HALVES, CHUNK], F32, name="out_t%d" % c, tag="out_t")
-            blender.tensor_tensor(out=out_t[c][:], in0=hid_t[c][:], in1=gate_t[(c, GATE_N)][:], op=ALU.subtract)
-            blender.tensor_tensor(out=out_t[c][:], in0=gate_t[(c, GATE_Z)][:], in1=out_t[c][:], op=ALU.mult)
-            blender.tensor_tensor(out=out_t[c][:], in0=gate_t[(c, GATE_N)][:], in1=out_t[c][:], op=ALU.add)
-
-        for c in range(N_CHUNKS - BLEND_LAG, N_CHUNKS):
-            for pair in range(PAIRS):
-                out_bank = psum_tr.tile([P, 2, N_HID], F32, name="out_bank", tag="bank")
-                for k in range(2):
-                    transpose_out_tile(c, 2 * pair + k, out_bank)
-                keep_out_pair(c, pair, out_bank)
+            if c < LAST - 1:
+                blend(c, nc.gpsimd, slice(0, 2))
+            elif c == LAST - 1:
+                blend(c, nc.gpsimd, slice(0, 1))
+                blend(c, nc.gpsimd, slice(1, 2))
+            else:
+                def send_half(cc, j):
+                    out_bank = psum_tr.tile([P, TILES, P], F32, name="out_bank", tag="bank")
+                    for s in range(TILES):
+                        nc.tensor.transpose(
+                            out=out_bank[:, s, :],
+                            in_=out_t[cc][:, j, P * s : P * (s + 1)],
+                            identity=ident_f32[:],
+                        )
+                    columns = slice(P * j, P * (j + 1))
+                    nc.scalar.copy(out=out_rows[cc][:, :, columns], in_=out_bank[:])
+                    nc.sync.dma_start(out=out_chunks[cc][:, :, columns], in_=out_rows[cc][:, :, columns])
+                for cc in (c - 1, c):
+                    out_rows[cc] = work.tile([P, TILES, N_HID], F32, name="out_rows%d" % cc, tag="out_rows")
+                for j in range(HALVES):
+                    send_half(c - 1, j)
+                for j in range(HALVES):
+                    blend(c, nc.vector, slice(j, j + 1))
+                    send_half(c, j)

@@ -222,6 +222,22 @@ def tile_grucellv2_t_e_kernel(tc, x, hid, wx_words, wx_scales, wh, bx, bh, out):
                 bias=bias_column(gate, j),
             )
 
+        def blend2(c, engine, part):
+            engine.tensor_tensor(out=out_t[c][:, part, :], in0=hid_t[c][:, part, :], in1=gate_t[(c, GATE_N)][:, part, :], op=ALU.subtract)
+            engine.tensor_tensor(out=out_t[c][:, part, :], in0=gate_t[(c, GATE_Z)][:, part, :], in1=out_t[c][:, part, :], op=ALU.mult)
+
+        def transpose_sum(first, second, s, half, place):
+            columns = slice(P * s, P * (s + 1))
+            for k, addend in enumerate((first, second)):
+                nc.tensor.matmul(
+                    out=place,
+                    lhsT=addend[:, half, columns],
+                    rhs=ident_f32[:],
+                    is_transpose=True,
+                    start=(k == 0),
+                    stop=(k == 1),
+                )
+
         def blend(c, engine, part):
             engine.tensor_tensor(out=out_t[c][:, part, :], in0=hid_t[c][:, part, :], in1=gate_t[(c, GATE_N)][:, part, :], op=ALU.subtract)
             engine.tensor_tensor(out=out_t[c][:, part, :], in0=gate_t[(c, GATE_Z)][:, part, :], in1=out_t[c][:, part, :], op=ALU.mult)
@@ -315,8 +331,18 @@ def tile_grucellv2_t_e_kernel(tc, x, hid, wx_words, wx_scales, wh, bx, bh, out):
 
                 for j in range(HALVES):
                     activate_half(c, gate, j)
-                if gate in weave_x:
-                    quantise_x(ahead, weave_x[gate])
+                if c == LAST and gate == GATE_Z:
+                    zc = work.tile([P, HALVES, CHUNK], F32, name="zc", tag="gate_zc", bufs=1)
+                    zh = work.tile([P, HALVES, CHUNK], F32, name="zh", tag="gate_zh", bufs=1)
+                    for j in range(HALVES):
+                        nc.scalar.activation(out=zc[:, j, :], in_=gate_t[(c, GATE_Z)][:, j, :], func=ACT.Identity, bias=1.0, scale=-1.0)
+                        nc.gpsimd.tensor_tensor(out=zh[:, j, :], in0=gate_t[(c, GATE_Z)][:, j, :], in1=hid_t[c][:, j, :], op=ALU.mult)
+                if c == 0:
+                    if gate in weave_x:
+                        quantise_x(ahead, weave_x[gate])
+                elif ahead < N_CHUNKS:
+                    for g in {GATE_Z: (0,), GATE_N: (1,)}.get(gate, ()):
+                        quantise_x(ahead, g)
                 if c == 0 and gate == GATE_N:
                     quantise_x(1, 1)
 
@@ -324,17 +350,13 @@ def tile_grucellv2_t_e_kernel(tc, x, hid, wx_words, wx_scales, wh, bx, bh, out):
             if c < LAST - 1:
                 blend(c, nc.gpsimd, slice(0, 2))
             elif c == LAST - 1:
-                blend(c, nc.gpsimd, slice(0, 1))
-                blend(c, nc.gpsimd, slice(1, 2))
+                blend2(c, nc.gpsimd, slice(0, 1))
+                blend2(c, nc.gpsimd, slice(1, 2))
             else:
                 def send_half(cc, j):
                     out_bank = psum_tr.tile([P, TILES, P], F32, name="out_bank", tag="bank")
                     for s in range(TILES):
-                        nc.tensor.transpose(
-                            out=out_bank[:, s, :],
-                            in_=out_t[cc][:, j, P * s : P * (s + 1)],
-                            identity=ident_f32[:],
-                        )
+                        transpose_sum(zh if cc == LAST else gate_t[(cc, GATE_N)], out_t[cc], s, j, out_bank[:, s, :])
                     columns = slice(P * j, P * (j + 1))
                     nc.scalar.copy(out=out_rows[cc][:, :, columns], in_=out_bank[:])
                     nc.sync.dma_start(out=out_chunks[cc][:, :, columns], in_=out_rows[cc][:, :, columns])
@@ -343,5 +365,5 @@ def tile_grucellv2_t_e_kernel(tc, x, hid, wx_words, wx_scales, wh, bx, bh, out):
                 for j in range(HALVES):
                     send_half(c - 1, j)
                 for j in range(HALVES):
-                    blend(c, nc.vector, slice(j, j + 1))
+                    nc.vector.tensor_tensor(out=out_t[c][:, j, :], in0=zc[:, j, :], in1=gate_t[(c, GATE_N)][:, j, :], op=ALU.mult)
                     send_half(c, j)

@@ -72,6 +72,10 @@ def tile_grucellv2_t_e_kernel(tc, x, hid, wx_words, wx_scales, wh, bx, bh, out):
                 in_=wx_words[groups].rearrange("g p n t -> p g (n t)").bitcast(I32),
             )
 
+        warm_rhs = consts.tile([P, CHUNK], BF16)
+        nc.vector.memset(warm_rhs[:], 0.0)
+        first_sigmoid = consts.tile([P, 1], F32)
+        nc.scalar.activation(out=first_sigmoid[:], in_=warm_rhs[:, 0:1], func=ACT.Sigmoid)
         bias_rows = consts.tile([P, P], BF16)
         nc.vector.memset(bias_rows[:], 0.0)
 
@@ -83,6 +87,11 @@ def tile_grucellv2_t_e_kernel(tc, x, hid, wx_words, wx_scales, wh, bx, bh, out):
         nc.vector.memset(w_scales[:].rearrange("p g n -> p (g n)").bitcast(I32), 0)
         w_codes = consts.tile([P, GATES * X_PASSES, N_HID], U32, align_bytes=64)
         wh_sb = consts.tile([P, GATES * HALVES, N_HID], BF16)
+
+        def load_wh(gate):
+            nc.sync.dma_start(
+                out=wh_sb[:, HALVES * gate : HALVES * (gate + 1), :], in_=wh[gate].rearrange("(k p) n -> p k n", p=P)
+            )
 
         def load_scales():
             for quadrant in range(4):
@@ -96,18 +105,21 @@ def tile_grucellv2_t_e_kernel(tc, x, hid, wx_words, wx_scales, wh, bx, bh, out):
         for g in range(X_PASSES):
             for pair in range(PAIRS):
                 load_x_part(0, g, pair)
-        nc.sync.dma_start(out=wh_sb[:], in_=wh.rearrange("g (k p) n -> p (g k) n", p=P))
+        load_wh(GATE_R)
+        load_wh(GATE_Z)
         load_codes(GATE_R)
         load_scales()
         load_biases()
-        load_codes(GATE_Z)
         load_hid(1)
+        load_codes(GATE_Z)
+        load_wh(GATE_N)
         load_x(1)
         load_codes(GATE_N)
 
         for c in range(2, N_CHUNKS):
             load_hid(c)
             load_x(c)
+
 
         ident_bf16 = consts.tile([P, P], BF16)
         make_identity(nc, ident_bf16[:])
@@ -169,8 +181,8 @@ def tile_grucellv2_t_e_kernel(tc, x, hid, wx_words, wx_scales, wh, bx, bh, out):
             column = HALVES * gate + j
             return (bias_x if gate == GATE_N else bias_sum)[:, column : column + 1]
 
-        def plain_half(c, gate, j, behind_matmul):
-            bank = psum_mm.tile([P, CHUNK], F32, name="h_sum", tag="h_sum")
+        def plain_half(c, gate, j, behind_matmul, tag="h_sum"):
+            bank = psum_mm.tile([P, CHUNK], F32, name=tag, tag=tag)
             for k in range(HALVES):
                 nc.tensor.matmul(
                     out=bank[:],
@@ -197,8 +209,8 @@ def tile_grucellv2_t_e_kernel(tc, x, hid, wx_words, wx_scales, wh, bx, bh, out):
                 copy(out=part[:], in_=bank[:])
             return part
 
-        def mx_half(c, gate, j):
-            bank = psum_mm.tile([P, CHUNK], F32, name="x_sum", tag="x_sum")
+        def mx_half(c, gate, j, tag="x_sum"):
+            bank = psum_mm.tile([P, CHUNK], F32, name=tag, tag=tag)
             for g in range(X_PASSES):
                 nc.tensor.matmul_mx(
                     out=bank[:],
@@ -251,19 +263,42 @@ def tile_grucellv2_t_e_kernel(tc, x, hid, wx_words, wx_scales, wh, bx, bh, out):
             nc.sync.dma_start(out=out_chunks[c][:, rows, :], in_=out_rows[c][:, rows, :])
 
         V, S = nc.vector.tensor_copy, nc.scalar.copy
+        warm_bank = psum_mm.tile([P, CHUNK], F32, name="warm_bank", tag="x_sum")
+
+        def warm(times):
+            for k in range(times):
+                nc.tensor.matmul(out=warm_bank[:], lhsT=warm_rhs[:, 0:P], rhs=warm_rhs[:], start=True, stop=True)
+
+        warm(3)
         begin_transposing(0)
         for s in range(TILES):
             for half in range(HALVES):
                 transpose_hid_tile(0, s, half)
-        keep_hid_t(0, S)
-        engines0 = (S, V, S, V)
-        for g in range(X_PASSES):
+        keep_hid_t(0, V)
+
+        def nothing(k):
+            return None
+
+        def x_run(c, g, engines):
             for pair in range(PAIRS):
                 x_bank = psum_tr.tile([P, 2, 2, P], F32, name="x_bank", tag="bank")
                 for k in range(2):
-                    transpose_x_tile(0, g, 2 * pair + k, x_bank)
-                regroup_x_pair(0, g, pair, x_bank, engines0[2 * g + pair])
-            quantise_x(0, g)
+                    transpose_x_tile(c, g, 2 * pair + k, x_bank)
+                regroup_x_pair(c, g, pair, x_bank, engines[pair])
+
+        for gate in range(GATES):
+            gate_t[(0, gate)] = work.tile([P, HALVES, CHUNK], F32, name="gate%d_0" % gate, tag="gate%d" % gate)
+        out_t[0] = work.tile([P, HALVES, CHUNK], F32, name="out_t0", tag="out_t")
+        x_run(0, 0, (S, V))
+        warm(1)
+        quantise_x(0, 0)
+        x_run(0, 1, (S, S))
+        warm(1)
+        h_r = [plain_half(0, GATE_R, j, nothing) for j in range(HALVES)]
+        p_r = [plain_part(0, GATE_R, j, h_r[j], (S, S)[j]) for j in range(HALVES)]
+        quantise_x(0, 1)
+        h_z = [plain_half(0, GATE_Z, j, nothing, "x_sum") for j in range(HALVES)]
+        p_z = [plain_part(0, GATE_Z, j, h_z[j], (V, S)[j]) for j in range(HALVES)]
         bias_bank = psum_tr.tile([P, P], BF16, name="bias_bank", tag="bank")
         nc.tensor.transpose(out=bias_bank[:], in_=bias_rows[:], identity=ident_bf16[:])
         bias = consts.tile([P, 2 * GATES * HALVES], F32)
@@ -273,8 +308,47 @@ def tile_grucellv2_t_e_kernel(tc, x, hid, wx_words, wx_scales, wh, bx, bh, out):
         bias_sum = consts.tile([P, GATES * HALVES], F32)
         nc.vector.tensor_add(out=bias_sum[:], in0=bias_x, in1=bias_h)
 
+        def mx_gate(gate, parts):
+            banks = []
+            for j in range(HALVES):
+                banks.append(mx_half(0, gate, j, "h_sum" if gate == GATE_R else "x_sum"))
+            return banks
+
+        def add_gate(gate, banks, parts):
+            for j in range(HALVES):
+                add_half(0, gate, j, banks[j], parts[j])
+
+        def act_gate(gate):
+            for j in range(HALVES):
+                activate_half(0, gate, j)
+
+        begin_transposing(1)
+        banks = mx_gate(GATE_R, p_r)
+        add_gate(GATE_R, banks, p_r)
+        act_gate(GATE_R)
+        for s in range(TILES):
+            for half in range(HALVES):
+                transpose_hid_tile(1, s, half)
+        keep_hid_t(1, S)
+        banks = mx_gate(GATE_Z, p_z)
+        add_gate(GATE_Z, banks, p_z)
+        act_gate(GATE_Z)
+        h_n = []
+        for j in range(HALVES):
+            x_bank = psum_tr.tile([P, 2, 2, P], F32, name="x_bank", tag="bank")
+            h_n.append(plain_half(0, GATE_N, j, lambda k: transpose_x_tile(1, 0, 2 * j + k, x_bank)))
+            regroup_x_pair(1, 0, j, x_bank, S)
+        p_n = [plain_part(0, GATE_N, j, h_n[j]) for j in range(HALVES)]
+        banks = mx_gate(GATE_N, p_n)
+        x_run(1, 1, (S, S))
+        add_gate(GATE_N, banks, p_n)
+        quantise_x(1, 0)
+        act_gate(GATE_N)
+        quantise_x(1, 1)
+        blend(0, nc.gpsimd, slice(0, 2))
+
         LAST = N_CHUNKS - 1
-        for c in range(N_CHUNKS):
+        for c in range(1, N_CHUNKS):
             ahead = c + 1
             if ahead < N_CHUNKS:
                 begin_transposing(ahead)

@@ -415,7 +415,7 @@ def tile_grucellv2_t_e_kernel(tc, x, hid, wx_words, wx_scales, wh, bx, bh, out):
                     if gate in weave_x:
                         quantise_x(ahead, weave_x[gate])
                 elif ahead < N_CHUNKS:
-                    for g in {GATE_Z: (0,), GATE_N: (1,)}.get(gate, ()):
+                    for g in {GATE_R: (0,), GATE_N: (1,)}.get(gate, ()):
                         quantise_x(ahead, g)
                 if c == 0 and gate == GATE_N:
                     quantise_x(1, 1)

@@ -57,13 +57,9 @@ def tile_grucellv2_t_e_kernel(tc, x, hid, wx_words, wx_scales, wh, bx, bh, out):
 
         def load_x(c):
             x_rows[c] = inputs.tile([P, TILES, N_IN], BF16, name="x_rows%d" % c, tag="x_rows")
-            for g in range(X_PASSES):
-                columns = slice(K_PASS * g, K_PASS * (g + 1))
-                nc.sync.dma_start(out=x_rows[c][:, :, columns], in_=x_chunks[c][:, :, columns])
-
-        def load_x_part(c, g, pair):
-            rows, columns = slice(2 * pair, 2 * pair + 2), slice(K_PASS * g, K_PASS * (g + 1))
-            nc.sync.dma_start(out=x_rows[c][:, rows, columns], in_=x_chunks[c][:, rows, columns])
+            for pair in range(PAIRS):
+                rows = slice(2 * pair, 2 * pair + 2)
+                nc.sync.dma_start(out=x_rows[c][:, rows, :], in_=x_chunks[c][:, rows, :])
 
         def load_codes(gate):
             groups = slice(X_PASSES * gate, X_PASSES * (gate + 1))
@@ -101,10 +97,7 @@ def tile_grucellv2_t_e_kernel(tc, x, hid, wx_words, wx_scales, wh, bx, bh, out):
                 )
 
         load_hid(0)
-        x_rows[0] = inputs.tile([P, TILES, N_IN], BF16, name="x_rows0", tag="x_rows")
-        for g in range(X_PASSES):
-            for pair in range(PAIRS):
-                load_x_part(0, g, pair)
+        load_x(0)
         load_wh(GATE_R)
         load_wh(GATE_Z)
         load_codes(GATE_R)
@@ -149,6 +142,14 @@ def tile_grucellv2_t_e_kernel(tc, x, hid, wx_words, wx_scales, wh, bx, bh, out):
             copy(
                 out=words.rearrange("p (k b u) -> p k b u", k=2, u=2),
                 in_=bank[:].rearrange("p k u b -> p k b u"),
+            )
+
+        def quantise_x_pair(c, g, pair):
+            columns = slice(256 * pair, 256 * (pair + 1))
+            nc.vector.quantize_mx(
+                out=x_codes[c][:, g, columns].bitcast(FP8X4),
+                scales=x_scales[c][:, g, columns],
+                in_=x_grouped[(c, g)][:, 1024 * pair : 1024 * (pair + 1)],
             )
 
         def quantise_x(c, g):
@@ -279,24 +280,20 @@ def tile_grucellv2_t_e_kernel(tc, x, hid, wx_words, wx_scales, wh, bx, bh, out):
         def nothing(k):
             return None
 
-        def x_run(c, g, engines):
-            for pair in range(PAIRS):
-                x_bank = psum_tr.tile([P, 2, 2, P], F32, name="x_bank", tag="bank")
-                for k in range(2):
-                    transpose_x_tile(c, g, 2 * pair + k, x_bank)
-                regroup_x_pair(c, g, pair, x_bank, engines[pair])
-
         for gate in range(GATES):
             gate_t[(0, gate)] = work.tile([P, HALVES, CHUNK], F32, name="gate%d_0" % gate, tag="gate%d" % gate)
         out_t[0] = work.tile([P, HALVES, CHUNK], F32, name="out_t0", tag="out_t")
-        x_run(0, 0, (S, V))
-        warm(1)
-        quantise_x(0, 0)
-        x_run(0, 1, (S, S))
-        warm(1)
+        for pair in range(PAIRS):
+            for g, copy in enumerate((S, V)):
+                x_bank = psum_tr.tile([P, 2, 2, P], F32, name="x_bank", tag="bank")
+                for k in range(2):
+                    transpose_x_tile(0, g, 2 * pair + k, x_bank)
+                regroup_x_pair(0, g, pair, x_bank, copy)
+            warm(1)
+            for g in range(X_PASSES):
+                quantise_x_pair(0, g, pair)
         h_r = [plain_half(0, GATE_R, j, nothing) for j in range(HALVES)]
         p_r = [plain_part(0, GATE_R, j, h_r[j], (S, S)[j]) for j in range(HALVES)]
-        quantise_x(0, 1)
         h_z = [plain_half(0, GATE_Z, j, nothing, "x_sum") for j in range(HALVES)]
         p_z = [plain_part(0, GATE_Z, j, h_z[j], (V, S)[j]) for j in range(HALVES)]
         bias_bank = psum_tr.tile([P, P], BF16, name="bias_bank", tag="bank")
@@ -336,15 +333,21 @@ def tile_grucellv2_t_e_kernel(tc, x, hid, wx_words, wx_scales, wh, bx, bh, out):
         h_n = []
         for j in range(HALVES):
             x_bank = psum_tr.tile([P, 2, 2, P], F32, name="x_bank", tag="bank")
-            h_n.append(plain_half(0, GATE_N, j, lambda k: transpose_x_tile(1, 0, 2 * j + k, x_bank)))
-            regroup_x_pair(1, 0, j, x_bank, S)
+            h_n.append(plain_half(0, GATE_N, j, lambda k: transpose_x_tile(1, j, k, x_bank)))
+            regroup_x_pair(1, j, 0, x_bank, S)
         p_n = [plain_part(0, GATE_N, j, h_n[j]) for j in range(HALVES)]
         banks = mx_gate(GATE_N, p_n)
-        x_run(1, 1, (S, S))
+        for g, copy in enumerate((S, S)):
+            x_bank = psum_tr.tile([P, 2, 2, P], F32, name="x_bank", tag="bank")
+            for k in range(2):
+                transpose_x_tile(1, g, 2 + k, x_bank)
+            regroup_x_pair(1, g, 1, x_bank, copy)
         add_gate(GATE_N, banks, p_n)
-        quantise_x(1, 0)
+        for g in range(X_PASSES):
+            quantise_x_pair(1, g, 0)
         act_gate(GATE_N)
-        quantise_x(1, 1)
+        for g in range(X_PASSES):
+            quantise_x_pair(1, g, 1)
         blend(0, nc.gpsimd, slice(0, 2))
 
         LAST = N_CHUNKS - 1

from contextlib import ExitStack

import concourse.mybir as mybir
from concourse.masks import make_identity

F32 = mybir.dt.float32
BF16 = mybir.dt.bfloat16
I32 = mybir.dt.int32
U32 = mybir.dt.uint32
U8 = mybir.dt.uint8
FP8X4 = mybir.dt.float8_e4m3fn_x4
ACT = mybir.ActivationFunctionType
ALU = mybir.AluOpType

P = 128
PACK = 4
K_PASS = P * PACK

BATCH, N_IN, N_HID = 4096, 1024, 256
GATE_R, GATE_Z, GATE_N = 0, 1, 2
GATES = 3
X_PASSES = N_IN // K_PASS
HALVES = N_HID // P
CHUNK = 512
TILES = CHUNK // P
N_CHUNKS = BATCH // CHUNK
PAIRS = TILES // 2
BLEND_LAG = 2

FLOPS = 2 * BATCH * (N_IN + N_HID) * GATES * N_HID


def tile_grucellv2_t_e_kernel(tc, x, hid, wx_words, wx_scales, wh, bx, bh, out):
    nc = tc.nc
    x_chunks = x.rearrange("(c p s) k -> c p s k", p=P, s=TILES)
    hid_chunks = hid.rearrange("(c p s) h -> c p s h", p=P, s=TILES)
    out_chunks = out.rearrange("(c p s) h -> c p s h", p=P, s=TILES)

    with ExitStack() as ctx:
        consts = ctx.enter_context(tc.tile_pool(name="consts", bufs=1))
        inputs = ctx.enter_context(tc.tile_pool(name="inputs", bufs=N_CHUNKS))
        work = ctx.enter_context(tc.tile_pool(name="work", bufs=3))
        psum_mm = ctx.enter_context(tc.psum_pool(name="psum_mm", bufs=2))
        psum_tr = ctx.enter_context(tc.psum_pool(name="psum_tr", bufs=3))
        psum_hid = ctx.enter_context(tc.psum_pool(name="psum_hid", bufs=1))
        ctx.enter_context(tc.manual_schedule())

        x_rows, hid_rows = {}, {}
        x_grouped, x_codes, x_scales = {}, {}, {}
        hid_bank, hid_t = {}, {}
        gate_t = {}
        out_t, out_rows = {}, {}

        def load_hid(c):
            hid_rows[c] = inputs.tile([P, TILES, N_HID], BF16, name="hid_rows%d" % c, tag="hid_rows")
            nc.sync.dma_start(out=hid_rows[c][:], in_=hid_chunks[c])

        def load_x(c):
            x_rows[c] = inputs.tile([P, TILES, N_IN], BF16, name="x_rows%d" % c, tag="x_rows")
            for pair in range(PAIRS):
                rows = slice(2 * pair, 2 * pair + 2)
                nc.sync.dma_start(out=x_rows[c][:, rows, :], in_=x_chunks[c][:, rows, :])

        def load_codes(gate):
            groups = slice(X_PASSES * gate, X_PASSES * (gate + 1))
            nc.sync.dma_start(
                out=w_codes[:, groups, :].bitcast(I32),
                in_=wx_words[groups].rearrange("g p n t -> p g (n t)").bitcast(I32),
            )

        warm_rhs = consts.tile([P, CHUNK], BF16)
        nc.vector.memset(warm_rhs[:], 0.0)
        first_sigmoid = consts.tile([P, 1], F32)
        nc.scalar.activation(out=first_sigmoid[:], in_=warm_rhs[:, 0:1], func=ACT.Sigmoid)
        bias_rows = consts.tile([P, P], BF16)
        nc.vector.memset(bias_rows[:], 0.0)

        def load_biases():
            nc.sync.dma_start(out=bias_rows[0:6, :], in_=bx.rearrange("g (j p) -> (g j) p", p=P))
            nc.sync.dma_start(out=bias_rows[6:12, :], in_=bh.rearrange("g (j p) -> (g j) p", p=P))

        w_scales = consts.tile([P, GATES * X_PASSES, N_HID], U8, align_bytes=64)
        nc.vector.memset(w_scales[:].rearrange("p g n -> p (g n)").bitcast(I32), 0)
        w_codes = consts.tile([P, GATES * X_PASSES, N_HID], U32, align_bytes=64)
        wh_sb = consts.tile([P, GATES * HALVES, N_HID], BF16)

        def load_wh(gate):
            nc.sync.dma_start(
                out=wh_sb[:, HALVES * gate : HALVES * (gate + 1), :], in_=wh[gate].rearrange("(k p) n -> p k n", p=P)
            )

        def load_scales():
            for quadrant in range(4):
                nc.sync.dma_start(
                    out=w_scales[32 * quadrant : 32 * quadrant + 4, :, :].bitcast(I32),
                    in_=wx_scales[:, 4 * quadrant : 4 * quadrant + 4, :].rearrange("g r n -> r g n").bitcast(I32),
                )

        load_hid(0)
        load_x(0)
        load_wh(GATE_R)
        load_wh(GATE_Z)
        load_codes(GATE_R)
        load_scales()
        load_biases()
        load_hid(1)
        load_codes(GATE_Z)
        load_wh(GATE_N)
        load_x(1)
        load_codes(GATE_N)

        for c in range(2, N_CHUNKS):
            load_hid(c)
            load_x(c)


        ident_bf16 = consts.tile([P, P], BF16)
        make_identity(nc, ident_bf16[:])
        ident_f32 = consts.tile([P, P], F32)
        make_identity(nc, ident_f32[:])

        def begin_transposing(c):
            x_codes[c] = work.tile([P, X_PASSES, CHUNK], U32, name="x_codes%d" % c, tag="x_codes", align_bytes=64)
            x_scales[c] = work.tile([P, X_PASSES, CHUNK], U8, name="x_scales%d" % c, tag="x_scales", align_bytes=64)
            hid_bank[c] = psum_hid.tile([P, HALVES, CHUNK], BF16, name="hid_bank%d" % c, tag="hid_bank")

        def transpose_x_tile(c, g, s, bank):
            words = x_rows[c][:].bitcast(F32)
            for u in range(2):
                nc.tensor.transpose(
                    out=bank[:, s % 2, u, :],
                    in_=words[:, s, 256 * g + u : 256 * (g + 1) : 2],
                    identity=ident_f32[:],
                )

        def regroup_x_pair(c, g, pair, bank, copy=nc.scalar.copy):
            if pair == 0:
                x_grouped[(c, g)] = work.tile(
                    [P, CHUNK * PACK], BF16, name="x_grouped%d_%d" % (c, g), tag="x_grouped", bufs=4, align_bytes=64
                )
            words = x_grouped[(c, g)][:].bitcast(F32)[:, 512 * pair : 512 * (pair + 1)]
            copy(
                out=words.rearrange("p (k b u) -> p k b u", k=2, u=2),
                in_=bank[:].rearrange("p k u b -> p k b u"),
            )

        def quantise_x_pair(c, g, pair):
            columns = slice(256 * pair, 256 * (pair + 1))
            nc.vector.quantize_mx(
                out=x_codes[c][:, g, columns].bitcast(FP8X4),
                scales=x_scales[c][:, g, columns],
                in_=x_grouped[(c, g)][:, 1024 * pair : 1024 * (pair + 1)],
            )

        def quantise_x(c, g):
            nc.vector.quantize_mx(
                out=x_codes[c][:, g, :].bitcast(FP8X4),
                scales=x_scales[c][:, g, :],
                in_=x_grouped[(c, g)][:],
            )

        def transpose_hid_tile(c, s, half):
            nc.tensor.transpose(
                out=hid_bank[c][:, half, P * s : P * (s + 1)],
                in_=hid_rows[c][:, s, P * half : P * (half + 1)],
                identity=ident_bf16[:],
            )

        def keep_hid_t(c, copy=nc.scalar.copy):
            hid_t[c] = work.tile([P, HALVES, CHUNK], BF16, name="hid_t%d" % c, tag="hid_t", bufs=4)
            copy(out=hid_t[c][:], in_=hid_bank[c][:])

        def transpose_out_tile(c, s, bank):
            for half in range(HALVES):
                nc.tensor.transpose(
                    out=bank[:, s % 2, P * half : P * (half + 1)],
                    in_=out_t[c][:, half, P * s : P * (s + 1)],
                    identity=ident_f32[:],
                )

        def bias_column(gate, j):
            column = HALVES * gate + j
            return (bias_x if gate == GATE_N else bias_sum)[:, column : column + 1]

        def plain_half(c, gate, j, behind_matmul, tag="h_sum"):
            bank = psum_mm.tile([P, CHUNK], F32, name=tag, tag=tag)
            for k in range(HALVES):
                nc.tensor.matmul(
                    out=bank[:],
                    lhsT=wh_sb[:, HALVES * gate + k, P * j : P * (j + 1)],
                    rhs=hid_t[c][:, k, :],
                    start=(k == 0),
                    stop=(k == HALVES - 1),
                )
                behind_matmul(k)
            return bank

        def plain_part(c, gate, j, bank, copy=nc.vector.tensor_copy):
            part = work.tile([P, CHUNK], F32, name="h_part", tag="h_part", bufs=4)
            if gate == GATE_N:
                nc.vector.scalar_tensor_tensor(
                    out=part[:],
                    in0=bank[:],
                    scalar=bias_h[:, HALVES * GATE_N + j : HALVES * GATE_N + j + 1],
                    in1=gate_t[(c, GATE_R)][:, j, :],
                    op0=ALU.add,
                    op1=ALU.mult,
                )
            else:
                copy(out=part[:], in_=bank[:])
            return part

        def mx_half(c, gate, j, tag="x_sum"):
            bank = psum_mm.tile([P, CHUNK], F32, name=tag, tag=tag)
            for g in range(X_PASSES):
                nc.tensor.matmul_mx(
                    out=bank[:],
                    lhsT=w_codes[:, X_PASSES * gate + g, P * j : P * (j + 1)].bitcast(FP8X4),
                    lhsT_scale=w_scales[:, X_PASSES * gate + g, P * j : P * (j + 1)],
                    rhs=x_codes[c][:, g, :].bitcast(FP8X4),
                    rhs_scale=x_scales[c][:, g, :],
                    start=(g == 0),
                    stop=(g == X_PASSES - 1),
                )
            return bank

        def add_half(c, gate, j, bank, part):
            nc.vector.tensor_tensor(out=gate_t[(c, gate)][:, j, :], in0=bank[:], in1=part[:], op=ALU.add)

        def activate_half(c, gate, j):
            nc.scalar.activation(
                out=gate_t[(c, gate)][:, j, :],
                in_=gate_t[(c, gate)][:, j, :],
                func=ACT.Tanh if gate == GATE_N else ACT.Sigmoid,
                bias=bias_column(gate, j),
            )

        def blend2(c, engine, part):
            engine.tensor_tensor(out=out_t[c][:, part, :], in0=hid_t[c][:, part, :], in1=gate_t[(c, GATE_N)][:, part, :], op=ALU.subtract)
            engine.tensor_tensor(out=out_t[c][:, part, :], in0=gate_t[(c, GATE_Z)][:, part, :], in1=out_t[c][:, part, :], op=ALU.mult)

        def transpose_sum(first, second, s, half, place):
            columns = slice(P * s, P * (s + 1))
            for k, addend in enumerate((first, second)):
                nc.tensor.matmul(
                    out=place,
                    lhsT=addend[:, half, columns],
                    rhs=ident_f32[:],
                    is_transpose=True,
                    start=(k == 0),
                    stop=(k == 1),
                )

        def blend(c, engine, part):
            engine.tensor_tensor(out=out_t[c][:, part, :], in0=hid_t[c][:, part, :], in1=gate_t[(c, GATE_N)][:, part, :], op=ALU.subtract)
            engine.tensor_tensor(out=out_t[c][:, part, :], in0=gate_t[(c, GATE_Z)][:, part, :], in1=out_t[c][:, part, :], op=ALU.mult)
            engine.tensor_tensor(out=out_t[c][:, part, :], in0=gate_t[(c, GATE_N)][:, part, :], in1=out_t[c][:, part, :], op=ALU.add)

        def keep_out_pair(c, pair, bank):
            if pair == 0:
                out_rows[c] = work.tile([P, TILES, N_HID], F32, name="out_rows%d" % c, tag="out_rows")
            rows = slice(2 * pair, 2 * pair + 2)
            nc.scalar.copy(out=out_rows[c][:, rows, :], in_=bank[:])
            nc.sync.dma_start(out=out_chunks[c][:, rows, :], in_=out_rows[c][:, rows, :])

        V, S = nc.vector.tensor_copy, nc.scalar.copy
        warm_bank = psum_mm.tile([P, CHUNK], F32, name="warm_bank", tag="x_sum")

        def warm(times):
            for k in range(times):
                nc.tensor.matmul(out=warm_bank[:], lhsT=warm_rhs[:, 0:P], rhs=warm_rhs[:], start=True, stop=True)

        warm(3)
        begin_transposing(0)
        for s in range(TILES):
            for half in range(HALVES):
                transpose_hid_tile(0, s, half)
        keep_hid_t(0, V)

        def nothing(k):
            return None

        for gate in range(GATES):
            gate_t[(0, gate)] = work.tile([P, HALVES, CHUNK], F32, name="gate%d_0" % gate, tag="gate%d" % gate)
        out_t[0] = work.tile([P, HALVES, CHUNK], F32, name="out_t0", tag="out_t")
        for pair in range(PAIRS):
            for g, copy in enumerate((S, V)):
                x_bank = psum_tr.tile([P, 2, 2, P], F32, name="x_bank", tag="bank")
                for k in range(2):
                    transpose_x_tile(0, g, 2 * pair + k, x_bank)
                regroup_x_pair(0, g, pair, x_bank, copy)
            warm(1)
            for g in range(X_PASSES):
                quantise_x_pair(0, g, pair)
        h_r = [plain_half(0, GATE_R, j, nothing) for j in range(HALVES)]
        p_r = [plain_part(0, GATE_R, j, h_r[j], (S, S)[j]) for j in range(HALVES)]
        h_z = [plain_half(0, GATE_Z, j, nothing, "x_sum") for j in range(HALVES)]
        p_z = [plain_part(0, GATE_Z, j, h_z[j], (V, S)[j]) for j in range(HALVES)]
        bias_bank = psum_tr.tile([P, P], BF16, name="bias_bank", tag="bank")
        nc.tensor.transpose(out=bias_bank[:], in_=bias_rows[:], identity=ident_bf16[:])
        bias = consts.tile([P, 2 * GATES * HALVES], F32)
        nc.vector.tensor_copy(out=bias[:], in_=bias_bank[:, 0 : 2 * GATES * HALVES])
        bias_x = bias[:, 0 : GATES * HALVES]
        bias_h = bias[:, GATES * HALVES : 2 * GATES * HALVES]
        bias_sum = consts.tile([P, GATES * HALVES], F32)
        nc.vector.tensor_add(out=bias_sum[:], in0=bias_x, in1=bias_h)

        def mx_gate(gate, parts):
            banks = []
            for j in range(HALVES):
                banks.append(mx_half(0, gate, j, "h_sum" if gate == GATE_R else "x_sum"))
            return banks

        def add_gate(gate, banks, parts):
            for j in range(HALVES):
                add_half(0, gate, j, banks[j], parts[j])

        def act_gate(gate):
            for j in range(HALVES):
                activate_half(0, gate, j)

        begin_transposing(1)
        banks = mx_gate(GATE_R, p_r)
        add_gate(GATE_R, banks, p_r)
        act_gate(GATE_R)
        for s in range(TILES):
            for half in range(HALVES):
                transpose_hid_tile(1, s, half)
        keep_hid_t(1, S)
        banks = mx_gate(GATE_Z, p_z)
        add_gate(GATE_Z, banks, p_z)
        act_gate(GATE_Z)
        h_n = []
        for j in range(HALVES):
            x_bank = psum_tr.tile([P, 2, 2, P], F32, name="x_bank", tag="bank")
            h_n.append(plain_half(0, GATE_N, j, lambda k: transpose_x_tile(1, j, k, x_bank)))
            regroup_x_pair(1, j, 0, x_bank, S)
        p_n = [plain_part(0, GATE_N, j, h_n[j]) for j in range(HALVES)]
        banks = mx_gate(GATE_N, p_n)
        for g, copy in enumerate((S, S)):
            x_bank = psum_tr.tile([P, 2, 2, P], F32, name="x_bank", tag="bank")
            for k in range(2):
                transpose_x_tile(1, g, 2 + k, x_bank)
            regroup_x_pair(1, g, 1, x_bank, copy)
        add_gate(GATE_N, banks, p_n)
        for g in range(X_PASSES):
            quantise_x_pair(1, g, 0)
        act_gate(GATE_N)
        for g in range(X_PASSES):
            quantise_x_pair(1, g, 1)
        blend(0, nc.gpsimd, slice(0, 2))

        LAST = N_CHUNKS - 1
        for c in range(1, N_CHUNKS):
            ahead = c + 1
            if ahead < N_CHUNKS:
                begin_transposing(ahead)
            weave_x = {GATE_N: 0} if c == 0 else {GATE_R: 0, GATE_Z: 1}
            weave_hid = {GATE_Z: (0, 1)} if c == 0 else {GATE_R: (0,), GATE_Z: (1,)}
            if ahead >= N_CHUNKS:
                weave_x, weave_hid = {}, {}
            weave_out = {GATE_N: c - BLEND_LAG}
            if c == LAST:
                weave_out = {GATE_Z: c - 2}
            for gate in range(GATES):
                gate_t[(c, gate)] = work.tile([P, HALVES, CHUNK], F32, name="gate%d_%d" % (gate, c), tag="gate%d" % gate)
                h_sum, x_sum, h_part = [], [], []
                back = weave_out.get(gate, -1)
                mx_first = False
                if mx_first:
                    for j in range(HALVES):
                        x_sum.append(mx_half(c, gate, j))
                for j in range(HALVES):
                    x_bank = out_bank = None
                    if gate in weave_x:
                        x_bank = psum_tr.tile([P, 2, 2, P], F32, name="x_bank", tag="bank")
                    if back >= 0:
                        out_bank = psum_tr.tile([P, 2, N_HID], F32, name="out_bank", tag="bank")

                    def behind_matmul(k):
                        if gate in weave_x:
                            transpose_x_tile(ahead, weave_x[gate], 2 * j + k, x_bank)
                        for i in weave_hid.get(gate, ()):
                            transpose_hid_tile(ahead, 2 * i + j, k)
                        if back >= 0:
                            transpose_out_tile(back, 2 * j + k, out_bank)

                    h_sum.append(plain_half(c, gate, j, behind_matmul))
                    if gate in weave_x:
                        regroup_x_pair(ahead, weave_x[gate], j, x_bank)
                    if back >= 0:
                        keep_out_pair(back, j, out_bank)
                for j in range(HALVES):
                    h_part.append(plain_part(c, gate, j, h_sum[j], S if c == 0 and gate in (GATE_R,) else V))
                if gate == GATE_Z and ahead < N_CHUNKS:
                    keep_hid_t(ahead)
                if not mx_first:
                    for j in range(HALVES):
                        x_sum.append(mx_half(c, gate, j))
                if c == 0 and gate == GATE_N:
                    for pair in range(PAIRS):
                        x_bank = psum_tr.tile([P, 2, 2, P], F32, name="x_bank", tag="bank")
                        for k in range(2):
                            transpose_x_tile(1, 1, 2 * pair + k, x_bank)
                        regroup_x_pair(1, 1, pair, x_bank, S)
                for j in range(HALVES):
                    add_half(c, gate, j, x_sum[j], h_part[j])

                for j in range(HALVES):
                    activate_half(c, gate, j)
                if c == LAST and gate == GATE_Z:
                    zc = work.tile([P, HALVES, CHUNK], F32, name="zc", tag="gate_zc", bufs=1)
                    zh = work.tile([P, HALVES, CHUNK], F32, name="zh", tag="gate_zh", bufs=1)
                    for j in range(HALVES):
                        nc.scalar.activation(out=zc[:, j, :], in_=gate_t[(c, GATE_Z)][:, j, :], func=ACT.Identity, bias=1.0, scale=-1.0)
                        nc.gpsimd.tensor_tensor(out=zh[:, j, :], in0=gate_t[(c, GATE_Z)][:, j, :], in1=hid_t[c][:, j, :], op=ALU.mult)
                if c == 0:
                    if gate in weave_x:
                        quantise_x(ahead, weave_x[gate])
                elif ahead < N_CHUNKS:
                    for g in {GATE_R: (0,), GATE_N: (1,)}.get(gate, ()):
                        quantise_x(ahead, g)
                if c == 0 and gate == GATE_N:
                    quantise_x(1, 1)

            out_t[c] = work.tile([P, HALVES, CHUNK], F32, name="out_t%d" % c, tag="out_t")
            if c < LAST - 1:
                blend(c, nc.gpsimd, slice(0, 2))
            elif c == LAST - 1:
                blend2(c, nc.gpsimd, slice(0, 1))
                blend2(c, nc.gpsimd, slice(1, 2))
            else:
                def send_half(cc, j):
                    out_bank = psum_tr.tile([P, TILES, P], F32, name="out_bank", tag="bank")
                    for s in range(TILES):
                        transpose_sum(zh if cc == LAST else gate_t[(cc, GATE_N)], out_t[cc], s, j, out_bank[:, s, :])
                    columns = slice(P * j, P * (j + 1))
                    nc.scalar.copy(out=out_rows[cc][:, :, columns], in_=out_bank[:])
                    nc.sync.dma_start(out=out_chunks[cc][:, :, columns], in_=out_rows[cc][:, :, columns])
                for cc in (c - 1, c):
                    out_rows[cc] = work.tile([P, TILES, N_HID], F32, name="out_rows%d" % cc, tag="out_rows")
                for j in range(HALVES):
                    send_half(c - 1, j)
                for j in range(HALVES):
                    nc.vector.tensor_tensor(out=out_t[c][:, j, :], in0=zc[:, j, :], in1=gate_t[(c, GATE_N)][:, j, :], op=ALU.mult)
                    send_half(c, j)
